import numpy as np
import ml_dtypes


def mxq(x, axis, fmt="e4m3"):
    dtype, down = {"e4m3": (ml_dtypes.float8_e4m3fn, 7), "e5m2": (ml_dtypes.float8_e5m2, 14)}[fmt]
    v = np.moveaxis(np.asarray(x, np.float32).astype(ml_dtypes.bfloat16).astype(np.float64), axis, -1)
    blocks = v.reshape(v.shape[:-1] + (-1, 32))
    amax = np.abs(blocks).max(-1, keepdims=True)
    byte = np.maximum(np.where(amax > 0, np.frexp(amax)[1] - 1 + 127, 0) - down, 1)
    scale = np.exp2(byte - 127.0)
    codes = (blocks / scale).astype(np.float32).astype(dtype).astype(np.float64)
    return np.moveaxis((codes * scale).reshape(v.shape), -1, axis)


WIDE = False


def mx_kscale(k):
    if not WIDE:
        return np.ones(k)
    levels = np.array([10, -10, 5, -5, 0])
    a = np.random.permutation(np.resize(levels, k // 512 * 4)).reshape(k // 512, 4)
    idx = np.arange(k)
    return np.exp2(a[idx // 512, idx % 128 // 32])


BF16 = ml_dtypes.bfloat16


def bf(x):
    return np.asarray(x, np.float32).astype(BF16)


def f64(x):
    return np.asarray(x).astype(np.float64)


B, D, T, DEPTH, LD = 8192, 1024, 128, 2, 128
NI = 2 ** DEPTH - 1
NL = 2 ** DEPTH


def sigmoid(v):
    return 1.0 / (1.0 + np.exp(-v))


def setup_inputs():
    s = mx_kscale(D)
    return {"x": bf(np.random.standard_normal((B, D)) * s),
            "W": bf(np.random.standard_normal((NI, T, D)) / np.sqrt(D) / s),
            "b": bf(np.random.standard_normal((NI, T)) * 0.5),
            "leaf_w": bf(np.random.standard_normal((NL, LD, T)) / np.sqrt(T * 0.6 ** DEPTH))}


def reference(x, W, b, leaf_w):
    wq = mxq(f64(W).reshape(NI * T, D), 1, "e4m3")
    z = (mxq(f64(x), 1, "e4m3") @ wq.T).reshape(B, NI, T) + f64(b)
    gates = sigmoid(z)
    probs = np.ones((B, 1, T))
    for l in range(DEPTH):
        g = gates[:, 2 ** l - 1: 2 ** (l + 1) - 1]
        probs = np.stack([probs * g, probs * (1.0 - g)], axis=2).reshape(B, 2 ** (l + 1), T)
    lw = f64(leaf_w).transpose(0, 2, 1).reshape(NL * T, LD)
    return mxq(probs.reshape(B, NL * T), 1, "e4m3") @ mxq(lw, 0, "e4m3")

@@ -1,0 +1,257 @@
+from contextlib import ExitStack
+
+import concourse.mybir as mybir
+from concourse.masks import make_identity
+
+BF16 = mybir.dt.bfloat16
+F32 = mybir.dt.float32
+U32 = mybir.dt.uint32
+U8 = mybir.dt.uint8
+FP8X4 = mybir.dt.float8_e4m3fn_x4
+SIGMOID = mybir.ActivationFunctionType.Sigmoid
+MULT = mybir.AluOpType.mult
+ADD = mybir.AluOpType.add
+
+P = 128
+BATCH, FEAT, TREES, NODES, LEAVES, OUTC = 8192, 1024, 128, 3, 4, 128
+ROWS = 4
+CHUNK = P * ROWS
+NCH = BATCH // CHUNK
+WORDS = FEAT // 2
+XBUFS = 8
+
+FLOPS = 2 * BATCH * FEAT * NODES * TREES + 2 * BATCH * LEAVES * TREES * OUTC
+
+
+def tile_softtreeensemble_pa_t_kernel(tc, x, W, b, leaf_w, out):
+    nc = tc.nc
+    with ExitStack() as ctx:
+        const = ctx.enter_context(tc.tile_pool(name="const", bufs=1))
+        xin = ctx.enter_context(tc.tile_pool(name="xin", bufs=XBUFS))
+        gxp = ctx.enter_context(tc.tile_pool(name="gxp", bufs=3))
+        xcp = ctx.enter_context(tc.tile_pool(name="xcp", bufs=2))
+        ghp = ctx.enter_context(tc.tile_pool(name="ghp", bufs=3))
+        pgp = ctx.enter_context(tc.tile_pool(name="pgp", bufs=2))
+        osb = ctx.enter_context(tc.tile_pool(name="osb", bufs=4))
+        tps = ctx.enter_context(tc.psum_pool(name="tps", bufs=4))
+        zps = ctx.enter_context(tc.psum_pool(name="zps", bufs=3))
+        ops = ctx.enter_context(tc.psum_pool(name="ops", bufs=1))
+        ctx.enter_context(tc.manual_schedule())
+
+        x_t, xt_t, gx_t, xc_t, z_t, gh_t, pg_t, pc_t, o_t = {}, {}, {}, {}, {}, {}, {}, {}, {}
+
+        def load_x(c):
+            x_sb = xin.tile([P, ROWS * FEAT], BF16, tag="x")
+            nc.sync.dma_start(
+                out=x_sb[:],
+                in_=x[c * CHUNK : (c + 1) * CHUNK, :].rearrange("(p r) d -> p (r d)", r=ROWS),
+            )
+            x_t[c] = x_sb
+
+        ident_f = const.tile([P, P], F32)
+        make_identity(nc, ident_f[:])
+        ident_b = const.tile([P, P], BF16)
+        make_identity(nc, ident_b[:])
+
+        warm_in = const.tile([P, 1], F32)
+        warm_out = const.tile([P, 1], F32)
+        nc.vector.memset(warm_in[:], 0.0)
+        b_sb = const.tile([P, P], BF16)
+        nc.vector.memset(b_sb[:], 0.0)
+
+        nc.scalar.dma_start(out=b_sb[0:NODES, :], in_=b)
+        l_sb = const.tile([P, LEAVES * TREES], BF16)
+        nc.scalar.dma_start(
+            out=l_sb[:].rearrange("c (j t) -> c j t", j=LEAVES),
+            in_=leaf_w.rearrange("j c t -> c j t"),
+        )
+        w_sb = const.tile([P, NODES * FEAT], BF16)
+        nc.sync.dma_start(
+            out=w_sb[:].rearrange("t (n d) -> t n d", n=NODES),
+            in_=W.rearrange("n t d -> t n d"),
+        )
+        for c in range(XBUFS):
+            load_x(c)
+
+        nc.scalar.activation(out=warm_out[:], in_=warm_in[:], func=SIGMOID)
+
+        bt = zps.tile([P, P], BF16, tag="z")
+        nc.tensor.transpose(bt[:], b_sb[:], ident_b[:])
+        bias = const.tile([P, NODES], F32)
+        nc.vector.tensor_copy(out=bias[:], in_=bt[:, 0:NODES])
+
+        lt = ops.tile([P, LEAVES, OUTC], BF16, tag="o")
+        for j in range(LEAVES):
+            nc.tensor.transpose(lt[:, j, :], l_sb[:, j * TREES : (j + 1) * TREES], ident_b[:])
+        lg = const.tile([P, OUTC * LEAVES], BF16, align_bytes=64)
+        nc.vector.tensor_copy(
+            out=lg[:].rearrange("p (c j) -> p c j", j=LEAVES),
+            in_=lt[:].rearrange("p j c -> p c j"),
+        )
+        lc = const.tile([P, OUTC], U32, align_bytes=64)
+        ls = const.tile([P, OUTC], U8, align_bytes=64)
+
+        ww = w_sb[:].bitcast(F32)
+        wg = const.tile([P, NODES * 512], F32, align_bytes=64)
+        wc = const.tile([P, NODES * 256], U32, align_bytes=64)
+        ws = const.tile([P, NODES * 256], U8, align_bytes=64)
+        for n in range(NODES):
+            wt = tps.tile([P, 4, P], F32, tag="xt")
+            for g in range(2):
+                for u in range(2):
+                    off = n * WORDS + 256 * g + 128 * u
+                    nc.tensor.transpose(wt[:, 2 * g + u, :], ww[:, off : off + P], ident_f[:])
+            nc.vector.tensor_copy(
+                out=wg[:, n * 512 : (n + 1) * 512].rearrange("p (g t u) -> p g t u", g=2, u=2),
+                in_=wt[:].rearrange("p (g u) t -> p g t u", u=2),
+            )
+        nc.vector.quantize_mx(out=lc[:].bitcast(FP8X4), scales=ls[:], in_=lg[:])
+        for n in range(NODES):
+            nc.vector.quantize_mx(
+                out=wc[:, n * 256 : (n + 1) * 256].bitcast(FP8X4),
+                scales=ws[:, n * 256 : (n + 1) * 256],
+                in_=wg[:].bitcast(BF16)[:, n * 1024 : (n + 1) * 1024],
+            )
+
+        def transposes(c):
+            xw = x_t[c][:].bitcast(F32)
+            banks = []
+            for g in range(2):
+                for h in range(2):
+                    xt = tps.tile([P, 2, 256], F32, tag="xt")
+                    for u in range(2):
+                        for q in range(2):
+                            off = (2 * h + q) * WORDS + 256 * g + 128 * u
+                            nc.tensor.transpose(
+                                xt[:, u, q * P : (q + 1) * P], xw[:, off : off + P], ident_f[:]
+                            )
+                    banks.append(xt)
+            xt_t[c] = banks
+
+        def leave_psum(c):
+            gx = gxp.tile([P, 2048], F32, tag="gx", align_bytes=64)
+            gx4 = gx[:].rearrange("p (g c u) -> p g c u", g=2, u=2)
+            for g in range(2):
+                for h in range(2):
+                    nc.scalar.copy(
+                        out=gx4[:, g, 256 * h : 256 * (h + 1), :],
+                        in_=xt_t[c][2 * g + h][:].rearrange("p u c -> p c u"),
+                    )
+            gx_t[c] = gx
+
+        def quantise_x(c):
+            xc = xcp.tile([P, 1024], U32, tag="xc", align_bytes=64)
+            xs = xcp.tile([P, 1024], U8, tag="xs", align_bytes=64)
+            nc.vector.quantize_mx(
+                out=xc[:].bitcast(FP8X4), scales=xs[:], in_=gx_t[c][:].bitcast(BF16)
+            )
+            xc_t[c] = (xc, xs)
+
+        def gates_matmul(c):
+            xc, xs = xc_t[c]
+            zs = []
+            for n in range(NODES):
+                z = zps.tile([P, CHUNK], F32, tag="z")
+                for g in range(2):
+                    wcol = slice((2 * n + g) * P, (2 * n + g + 1) * P)
+                    xcol = slice(g * CHUNK, (g + 1) * CHUNK)
+                    nc.tensor.matmul_mx(
+                        out=z[:],
+                        lhsT=wc[:, wcol].bitcast(FP8X4),
+                        lhsT_scale=ws[:, wcol],
+                        rhs=xc[:, xcol].bitcast(FP8X4),
+                        rhs_scale=xs[:, xcol],
+                        start=(g == 0),
+                        stop=(g == 1),
+                    )
+                zs.append(z)
+            z_t[c] = zs
+
+        def sigmoids(c):
+            gh = ghp.tile([P, 2 * NODES * CHUNK], F32, tag="gh")
+            for n in range(NODES):
+                nc.scalar.activation(
+                    out=gh[:, n * CHUNK : (n + 1) * CHUNK],
+                    in_=z_t[c][n][:],
+                    func=SIGMOID,
+                    bias=bias[:, n : n + 1],
+                    scale=1.0,
+                )
+            gh_t[c] = gh
+
+        def complements(c):
+            gh = gh_t[c]
+            half = NODES * CHUNK
+            nc.vector.tensor_scalar(
+                out=gh[:, half : 2 * half],
+                in0=gh[:, 0:half],
+                scalar1=-1.0,
+                scalar2=1.0,
+                op0=MULT,
+                op1=ADD,
+            )
+
+        def products(c):
+            gh4 = gh_t[c][:].rearrange("p (s n c) -> p s n c", s=2, n=NODES)
+            pg = pgp.tile([P, CHUNK * LEAVES], BF16, tag="pg", align_bytes=64)
+            nc.vector.tensor_tensor(
+                out=pg[:].rearrange("p (c a b) -> p c a b", a=2, b=2),
+                in0=gh4[:, :, 0:1, :].rearrange("p a o c -> p c a o").to_broadcast([P, CHUNK, 2, 2]),
+                in1=gh4[:, :, 1:3, :].rearrange("p b a c -> p c a b"),
+                op=MULT,
+            )
+            pg_t[c] = pg
+
+        def quantise_p(c):
+            pc = pgp.tile([P, CHUNK], U32, tag="pc", align_bytes=64)
+            ps = pgp.tile([P, CHUNK], U8, tag="ps", align_bytes=64)
+            nc.vector.quantize_mx(out=pc[:].bitcast(FP8X4), scales=ps[:], in_=pg_t[c][:])
+            pc_t[c] = (pc, ps)
+
+        def leaves_matmul(c):
+            pc, ps = pc_t[c]
+            o_ps = ops.tile([P, ROWS * OUTC], F32, tag="o")
+            for r in range(ROWS):
+                col = slice(r * P, (r + 1) * P)
+                nc.tensor.matmul_mx(
+                    out=o_ps[:, r * OUTC : (r + 1) * OUTC],
+                    lhsT=pc[:, col].bitcast(FP8X4),
+                    lhsT_scale=ps[:, col],
+                    rhs=lc[:].bitcast(FP8X4),
+                    rhs_scale=ls[:],
+                    start=True,
+                    stop=True,
+                )
+            o_t[c] = o_ps
+
+        def store(c):
+            o_sb = osb.tile([P, ROWS * OUTC], F32, tag="o_sb")
+            nc.scalar.copy(out=o_sb[:], in_=o_t[c][:])
+            nc.sync.dma_start(
+                out=out[c * CHUNK : (c + 1) * CHUNK, :].rearrange("(p r) c -> p (r c)", r=ROWS),
+                in_=o_sb[:],
+            )
+
+        def live(c):
+            return 0 <= c < NCH
+
+        for i in range(-3, NCH + 2):
+            if live(i):
+                complements(i)
+            if live(i + 1):
+                gates_matmul(i + 1)
+                sigmoids(i + 1)
+            if live(i - 1):
+                products(i - 1)
+            if live(i - 2):
+                leaves_matmul(i - 2)
+                store(i - 2)
+            if live(i + 3):
+                transposes(i + 3)
+                leave_psum(i + 3)
+                if live(i + 3 + XBUFS):
+                    load_x(i + 3 + XBUFS)
+            if live(i + 2):
+                quantise_x(i + 2)
+            if live(i - 1):
+                quantise_p(i - 1)

@@ -169,10 +169,13 @@ def tile_softtreeensemble_pa_t_kernel(tc, x, W, b, leaf_w, out):
 
         def sigmoids(c):
             gh = ghp.tile([P, 2 * NODES * CHUNK], F32, tag="gh")
+            lines = gh[:].rearrange("p (k i) -> p k i", i=4)
             for n in range(NODES):
+                first, step = ((0, 2), (256, 4), (258, 4))[n]
+                stop = 256 if n == 0 else 768
                 nc.scalar.activation(
-                    out=gh[:, n * CHUNK : (n + 1) * CHUNK],
-                    in_=z_t[c][n][:],
+                    out=lines[:, first:stop:step, :],
+                    in_=z_t[c][n][:].rearrange("p (k i) -> p k i", i=4),
                     func=SIGMOID,
                     bias=bias[:, n : n + 1],
                     scale=1.0,
@@ -180,11 +183,10 @@ def tile_softtreeensemble_pa_t_kernel(tc, x, W, b, leaf_w, out):
             gh_t[c] = gh
 
         def complements(c):
-            gh = gh_t[c]
-            half = NODES * CHUNK
+            pairs = gh_t[c][:].rearrange("p (k s i) -> p k s i", s=2, i=4)
             nc.vector.tensor_scalar(
-                out=gh[:, half : 2 * half],
-                in0=gh[:, 0:half],
+                out=pairs[:, :, 1:2, :],
+                in0=pairs[:, :, 0:1, :],
                 scalar1=-1.0,
                 scalar2=1.0,
                 op0=MULT,
@@ -192,12 +194,14 @@ def tile_softtreeensemble_pa_t_kernel(tc, x, W, b, leaf_w, out):
             )
 
         def products(c):
-            gh4 = gh_t[c][:].rearrange("p (s n c) -> p s n c", s=2, n=NODES)
+            gh = gh_t[c]
             pg = pgp.tile([P, CHUNK * LEAVES], BF16, tag="pg", align_bytes=64)
             nc.vector.tensor_tensor(
-                out=pg[:].rearrange("p (c a b) -> p c a b", a=2, b=2),
-                in0=gh4[:, :, 0:1, :].rearrange("p a o c -> p c a o").to_broadcast([P, CHUNK, 2, 2]),
-                in1=gh4[:, :, 1:3, :].rearrange("p b a c -> p c a b"),
+                out=pg[:].rearrange("p (k i a b) -> p k a b i", i=4, a=2, b=2),
+                in0=gh[:, 0 : 2 * CHUNK]
+                .rearrange("p (k a o i) -> p k a o i", a=2, o=1, i=4)
+                .to_broadcast([P, CHUNK // 4, 2, 2, 4]),
+                in1=gh[:, 2 * CHUNK : 6 * CHUNK].rearrange("p (k a b i) -> p k a b i", a=2, b=2, i=4),
                 op=MULT,
             )
             pg_t[c] = pg

@@ -59,37 +59,42 @@ def tile_softtreeensemble_pa_t_kernel(tc, x, W, b, leaf_w, out):
         b_sb = const.tile([P, P], BF16)
         nc.vector.memset(b_sb[:], 0.0)
 
-        nc.scalar.dma_start(out=b_sb[0:NODES, :], in_=b)
-        l_sb = const.tile([P, LEAVES * TREES], BF16)
-        nc.scalar.dma_start(
-            out=l_sb[:].rearrange("c (j t) -> c j t", j=LEAVES),
-            in_=leaf_w.rearrange("j c t -> c j t"),
-        )
         w_sb = const.tile([P, NODES * FEAT], BF16)
         nc.sync.dma_start(
             out=w_sb[:].rearrange("t (n d) -> t n d", n=NODES),
             in_=W.rearrange("n t d -> t n d"),
         )
-        for c in range(XBUFS):
+        load_x(0)
+        nc.sync.dma_start(out=b_sb[0:NODES, :], in_=b)
+        l_sb = const.tile([P, LEAVES * TREES], BF16)
+        nc.sync.dma_start(
+            out=l_sb[:].rearrange("c (j t) -> c j t", j=LEAVES),
+            in_=leaf_w.rearrange("j c t -> c j t"),
+        )
+        for c in range(1, XBUFS):
             load_x(c)
 
         nc.scalar.activation(out=warm_out[:], in_=warm_in[:], func=SIGMOID)
 
-        bt = zps.tile([P, P], BF16, tag="z")
-        nc.tensor.transpose(bt[:], b_sb[:], ident_b[:])
         bias = const.tile([P, NODES], F32)
-        nc.vector.tensor_copy(out=bias[:], in_=bt[:, 0:NODES])
-
-        lt = ops.tile([P, LEAVES, OUTC], BF16, tag="o")
-        for j in range(LEAVES):
-            nc.tensor.transpose(lt[:, j, :], l_sb[:, j * TREES : (j + 1) * TREES], ident_b[:])
         lg = const.tile([P, OUTC * LEAVES], BF16, align_bytes=64)
-        nc.vector.tensor_copy(
-            out=lg[:].rearrange("p (c j) -> p c j", j=LEAVES),
-            in_=lt[:].rearrange("p j c -> p c j"),
-        )
         lc = const.tile([P, OUTC], U32, align_bytes=64)
         ls = const.tile([P, OUTC], U8, align_bytes=64)
+
+        def prepare_bias():
+            bt = zps.tile([P, P], BF16, tag="z")
+            nc.tensor.transpose(bt[:], b_sb[:], ident_b[:])
+            nc.vector.tensor_copy(out=bias[:], in_=bt[:, 0:NODES])
+
+        def prepare_leaves():
+            lt = ops.tile([P, LEAVES, OUTC], BF16, tag="o")
+            for j in range(LEAVES):
+                nc.tensor.transpose(lt[:, j, :], l_sb[:, j * TREES : (j + 1) * TREES], ident_b[:])
+            nc.vector.tensor_copy(
+                out=lg[:].rearrange("p (c j) -> p c j", j=LEAVES),
+                in_=lt[:].rearrange("p j c -> p c j"),
+            )
+            nc.vector.quantize_mx(out=lc[:].bitcast(FP8X4), scales=ls[:], in_=lg[:])
 
         ww = w_sb[:].bitcast(F32)
         wg = const.tile([P, NODES * 512], F32, align_bytes=64)
@@ -105,7 +110,6 @@ def tile_softtreeensemble_pa_t_kernel(tc, x, W, b, leaf_w, out):
                 out=wg[:, n * 512 : (n + 1) * 512].rearrange("p (g t u) -> p g t u", g=2, u=2),
                 in_=wt[:].rearrange("p (g u) t -> p g t u", u=2),
             )
-        nc.vector.quantize_mx(out=lc[:].bitcast(FP8X4), scales=ls[:], in_=lg[:])
         for n in range(NODES):
             nc.vector.quantize_mx(
                 out=wc[:, n * 256 : (n + 1) * 256].bitcast(FP8X4),
@@ -240,22 +244,26 @@ def tile_softtreeensemble_pa_t_kernel(tc, x, W, b, leaf_w, out):
             return 0 <= c < NCH
 
         for i in range(-3, NCH + 2):
-            if live(i):
-                complements(i)
+            if live(i - 1):
+                products(i - 1)
             if live(i + 1):
                 gates_matmul(i + 1)
                 sigmoids(i + 1)
-            if live(i - 1):
-                products(i - 1)
-            if live(i - 2):
-                leaves_matmul(i - 2)
-                store(i - 2)
+            if live(i):
+                complements(i)
             if live(i + 3):
                 transposes(i + 3)
                 leave_psum(i + 3)
                 if live(i + 3 + XBUFS):
                     load_x(i + 3 + XBUFS)
+            if i == -3:
+                prepare_bias()
+            if live(i - 2):
+                leaves_matmul(i - 2)
+                store(i - 2)
             if live(i + 2):
                 quantise_x(i + 2)
+            if i == -1:
+                prepare_leaves()
             if live(i - 1):
                 quantise_p(i - 1)

@@ -19,6 +19,7 @@ CHUNK = P * ROWS
 NCH = BATCH // CHUNK
 WORDS = FEAT // 2
 XBUFS = 8
+ROOT_ON_SCALAR_FROM = 6
 
 FLOPS = 2 * BATCH * FEAT * NODES * TREES + 2 * BATCH * LEAVES * TREES * OUTC
 
@@ -36,7 +37,6 @@ def tile_softtreeensemble_pa_t_kernel(tc, x, W, b, leaf_w, out):
         tps = ctx.enter_context(tc.psum_pool(name="tps", bufs=4))
         zps = ctx.enter_context(tc.psum_pool(name="zps", bufs=3))
         ops = ctx.enter_context(tc.psum_pool(name="ops", bufs=1))
-        ctx.enter_context(tc.manual_schedule())
 
         x_t, xt_t, gx_t, xc_t, z_t, gh_t, pg_t, pc_t, o_t = {}, {}, {}, {}, {}, {}, {}, {}, {}
 
@@ -77,6 +77,7 @@ def tile_softtreeensemble_pa_t_kernel(tc, x, W, b, leaf_w, out):
         nc.scalar.activation(out=warm_out[:], in_=warm_in[:], func=SIGMOID)
 
         bias = const.tile([P, NODES], F32)
+        minus_bias = const.tile([P, NODES], F32)
         lg = const.tile([P, OUTC * LEAVES], BF16, align_bytes=64)
         lc = const.tile([P, OUTC], U32, align_bytes=64)
         ls = const.tile([P, OUTC], U8, align_bytes=64)
@@ -85,6 +86,9 @@ def tile_softtreeensemble_pa_t_kernel(tc, x, W, b, leaf_w, out):
             bt = zps.tile([P, P], BF16, tag="z")
             nc.tensor.transpose(bt[:], b_sb[:], ident_b[:])
             nc.vector.tensor_copy(out=bias[:], in_=bt[:, 0:NODES])
+            nc.vector.tensor_scalar(
+                out=minus_bias[:], in0=bt[:, 0:NODES], scalar1=-1.0, scalar2=None, op0=MULT
+            )
 
         def prepare_leaves():
             lt = ops.tile([P, LEAVES, OUTC], BF16, tag="o")
@@ -184,10 +188,19 @@ def tile_softtreeensemble_pa_t_kernel(tc, x, W, b, leaf_w, out):
                     bias=bias[:, n : n + 1],
                     scale=1.0,
                 )
+            if c >= ROOT_ON_SCALAR_FROM:
+                nc.scalar.activation(
+                    out=lines[:, 1:256:2, :],
+                    in_=z_t[c][0][:].rearrange("p (k i) -> p k i", i=4),
+                    func=SIGMOID,
+                    bias=minus_bias[:, 0:1],
+                    scale=-1.0,
+                )
             gh_t[c] = gh
 
         def complements(c):
-            pairs = gh_t[c][:].rearrange("p (k s i) -> p k s i", s=2, i=4)
+            first = 2 * CHUNK if c >= ROOT_ON_SCALAR_FROM else 0
+            pairs = gh_t[c][:, first : 6 * CHUNK].rearrange("p (k s i) -> p k s i", s=2, i=4)
             nc.vector.tensor_scalar(
                 out=pairs[:, :, 1:2, :],
                 in0=pairs[:, :, 0:1, :],

@@ -15,8 +15,9 @@ ADD = mybir.AluOpType.add
 P = 128
 BATCH, FEAT, TREES, NODES, LEAVES, OUTC = 8192, 1024, 128, 3, 4, 128
 ROWS = 4
-CHUNK = P * ROWS
-NCH = BATCH // CHUNK
+CHUNK_ROWS = [2] + [ROWS] * 15 + [2]
+NCH = len(CHUNK_ROWS)
+FIRST_ROW = [P * sum(CHUNK_ROWS[:c]) for c in range(NCH)]
 WORDS = FEAT // 2
 XBUFS = 8
 ROOT_ON_SCALAR_FROM = 6
@@ -41,10 +42,11 @@ def tile_softtreeensemble_pa_t_kernel(tc, x, W, b, leaf_w, out):
         x_t, xt_t, gx_t, xc_t, z_t, gh_t, pg_t, pc_t, o_t = {}, {}, {}, {}, {}, {}, {}, {}, {}
 
         def load_x(c):
-            x_sb = xin.tile([P, ROWS * FEAT], BF16, tag="x")
+            rows = CHUNK_ROWS[c]
+            x_sb = xin.tile([P, rows * FEAT], BF16, tag="x")
             nc.sync.dma_start(
                 out=x_sb[:],
-                in_=x[c * CHUNK : (c + 1) * CHUNK, :].rearrange("(p r) d -> p (r d)", r=ROWS),
+                in_=x[FIRST_ROW[c] : FIRST_ROW[c] + P * rows, :].rearrange("(p r) d -> p (r d)", r=rows),
             )
             x_t[c] = x_sb
 
@@ -60,10 +62,8 @@ def tile_softtreeensemble_pa_t_kernel(tc, x, W, b, leaf_w, out):
         nc.vector.memset(b_sb[:], 0.0)
 
         w_sb = const.tile([P, NODES * FEAT], BF16)
-        nc.sync.dma_start(
-            out=w_sb[:].rearrange("t (n d) -> t n d", n=NODES),
-            in_=W.rearrange("n t d -> t n d"),
-        )
+        for n in range(NODES):
+            nc.sync.dma_start(out=w_sb[:, n * FEAT : (n + 1) * FEAT], in_=W[n, :, :])
         load_x(0)
         nc.sync.dma_start(out=b_sb[0:NODES, :], in_=b)
         l_sb = const.tile([P, LEAVES * TREES], BF16)
@@ -125,7 +125,7 @@ def tile_softtreeensemble_pa_t_kernel(tc, x, W, b, leaf_w, out):
             xw = x_t[c][:].bitcast(F32)
             banks = []
             for g in range(2):
-                for h in range(2):
+                for h in range(CHUNK_ROWS[c] // 2):
                     xt = tps.tile([P, 2, 256], F32, tag="xt")
                     for u in range(2):
                         for q in range(2):
@@ -137,19 +137,21 @@ def tile_softtreeensemble_pa_t_kernel(tc, x, W, b, leaf_w, out):
             xt_t[c] = banks
 
         def leave_psum(c):
-            gx = gxp.tile([P, 2048], F32, tag="gx", align_bytes=64)
+            halves = CHUNK_ROWS[c] // 2
+            gx = gxp.tile([P, 1024 * halves], F32, tag="gx", align_bytes=64)
             gx4 = gx[:].rearrange("p (g c u) -> p g c u", g=2, u=2)
             for g in range(2):
-                for h in range(2):
+                for h in range(halves):
                     nc.scalar.copy(
                         out=gx4[:, g, 256 * h : 256 * (h + 1), :],
-                        in_=xt_t[c][2 * g + h][:].rearrange("p u c -> p c u"),
+                        in_=xt_t[c][halves * g + h][:].rearrange("p u c -> p c u"),
                     )
             gx_t[c] = gx
 
         def quantise_x(c):
-            xc = xcp.tile([P, 1024], U32, tag="xc", align_bytes=64)
-            xs = xcp.tile([P, 1024], U8, tag="xs", align_bytes=64)
+            cols = 2 * P * CHUNK_ROWS[c]
+            xc = xcp.tile([P, cols], U32, tag="xc", align_bytes=64)
+            xs = xcp.tile([P, cols], U8, tag="xs", align_bytes=64)
             nc.vector.quantize_mx(
                 out=xc[:].bitcast(FP8X4), scales=xs[:], in_=gx_t[c][:].bitcast(BF16)
             )
@@ -157,12 +159,13 @@ def tile_softtreeensemble_pa_t_kernel(tc, x, W, b, leaf_w, out):
 
         def gates_matmul(c):
             xc, xs = xc_t[c]
+            n_rows = P * CHUNK_ROWS[c]
             zs = []
             for n in range(NODES):
-                z = zps.tile([P, CHUNK], F32, tag="z")
+                z = zps.tile([P, n_rows], F32, tag="z")
                 for g in range(2):
                     wcol = slice((2 * n + g) * P, (2 * n + g + 1) * P)
-                    xcol = slice(g * CHUNK, (g + 1) * CHUNK)
+                    xcol = slice(g * n_rows, (g + 1) * n_rows)
                     nc.tensor.matmul_mx(
                         out=z[:],
                         lhsT=wc[:, wcol].bitcast(FP8X4),
@@ -176,11 +179,13 @@ def tile_softtreeensemble_pa_t_kernel(tc, x, W, b, leaf_w, out):
             z_t[c] = zs
 
         def sigmoids(c):
-            gh = ghp.tile([P, 2 * NODES * CHUNK], F32, tag="gh")
+            n_rows = P * CHUNK_ROWS[c]
+            half = n_rows // 2
+            gh = ghp.tile([P, 2 * NODES * n_rows], F32, tag="gh")
             lines = gh[:].rearrange("p (k i) -> p k i", i=4)
             for n in range(NODES):
-                first, step = ((0, 2), (256, 4), (258, 4))[n]
-                stop = 256 if n == 0 else 768
+                first, step = ((0, 2), (half, 4), (half + 2, 4))[n]
+                stop = half if n == 0 else 3 * half
                 nc.scalar.activation(
                     out=lines[:, first:stop:step, :],
                     in_=z_t[c][n][:].rearrange("p (k i) -> p k i", i=4),
@@ -190,7 +195,7 @@ def tile_softtreeensemble_pa_t_kernel(tc, x, W, b, leaf_w, out):
                 )
             if c >= ROOT_ON_SCALAR_FROM:
                 nc.scalar.activation(
-                    out=lines[:, 1:256:2, :],
+                    out=lines[:, 1:half:2, :],
                     in_=z_t[c][0][:].rearrange("p (k i) -> p k i", i=4),
                     func=SIGMOID,
                     bias=minus_bias[:, 0:1],
@@ -199,8 +204,9 @@ def tile_softtreeensemble_pa_t_kernel(tc, x, W, b, leaf_w, out):
             gh_t[c] = gh
 
         def complements(c):
-            first = 2 * CHUNK if c >= ROOT_ON_SCALAR_FROM else 0
-            pairs = gh_t[c][:, first : 6 * CHUNK].rearrange("p (k s i) -> p k s i", s=2, i=4)
+            n_rows = P * CHUNK_ROWS[c]
+            first = 2 * n_rows if c >= ROOT_ON_SCALAR_FROM else 0
+            pairs = gh_t[c][:, first : 6 * n_rows].rearrange("p (k s i) -> p k s i", s=2, i=4)
             nc.vector.tensor_scalar(
                 out=pairs[:, :, 1:2, :],
                 in0=pairs[:, :, 0:1, :],
@@ -212,27 +218,29 @@ def tile_softtreeensemble_pa_t_kernel(tc, x, W, b, leaf_w, out):
 
         def products(c):
             gh = gh_t[c]
-            pg = pgp.tile([P, CHUNK * LEAVES], BF16, tag="pg", align_bytes=64)
+            n_rows = P * CHUNK_ROWS[c]
+            pg = pgp.tile([P, n_rows * LEAVES], BF16, tag="pg", align_bytes=64)
             nc.vector.tensor_tensor(
                 out=pg[:].rearrange("p (k i a b) -> p k a b i", i=4, a=2, b=2),
-                in0=gh[:, 0 : 2 * CHUNK]
+                in0=gh[:, 0 : 2 * n_rows]
                 .rearrange("p (k a o i) -> p k a o i", a=2, o=1, i=4)
-                .to_broadcast([P, CHUNK // 4, 2, 2, 4]),
-                in1=gh[:, 2 * CHUNK : 6 * CHUNK].rearrange("p (k a b i) -> p k a b i", a=2, b=2, i=4),
+                .to_broadcast([P, n_rows // 4, 2, 2, 4]),
+                in1=gh[:, 2 * n_rows : 6 * n_rows].rearrange("p (k a b i) -> p k a b i", a=2, b=2, i=4),
                 op=MULT,
             )
             pg_t[c] = pg
 
         def quantise_p(c):
-            pc = pgp.tile([P, CHUNK], U32, tag="pc", align_bytes=64)
-            ps = pgp.tile([P, CHUNK], U8, tag="ps", align_bytes=64)
+            n_rows = P * CHUNK_ROWS[c]
+            pc = pgp.tile([P, n_rows], U32, tag="pc", align_bytes=64)
+            ps = pgp.tile([P, n_rows], U8, tag="ps", align_bytes=64)
             nc.vector.quantize_mx(out=pc[:].bitcast(FP8X4), scales=ps[:], in_=pg_t[c][:])
             pc_t[c] = (pc, ps)
 
         def leaves_matmul(c):
             pc, ps = pc_t[c]
-            o_ps = ops.tile([P, ROWS * OUTC], F32, tag="o")
-            for r in range(ROWS):
+            o_ps = ops.tile([P, CHUNK_ROWS[c] * OUTC], F32, tag="o")
+            for r in range(CHUNK_ROWS[c]):
                 col = slice(r * P, (r + 1) * P)
                 nc.tensor.matmul_mx(
                     out=o_ps[:, r * OUTC : (r + 1) * OUTC],
@@ -246,10 +254,11 @@ def tile_softtreeensemble_pa_t_kernel(tc, x, W, b, leaf_w, out):
             o_t[c] = o_ps
 
         def store(c):
-            o_sb = osb.tile([P, ROWS * OUTC], F32, tag="o_sb")
+            rows = CHUNK_ROWS[c]
+            o_sb = osb.tile([P, rows * OUTC], F32, tag="o_sb")
             nc.scalar.copy(out=o_sb[:], in_=o_t[c][:])
             nc.sync.dma_start(
-                out=out[c * CHUNK : (c + 1) * CHUNK, :].rearrange("(p r) c -> p (r c)", r=ROWS),
+                out=out[FIRST_ROW[c] : FIRST_ROW[c] + P * rows, :].rearrange("(p r) c -> p (r c)", r=rows),
                 in_=o_sb[:],
             )
 

@@ -20,7 +20,7 @@ NCH = len(CHUNK_ROWS)
 FIRST_ROW = [P * sum(CHUNK_ROWS[:c]) for c in range(NCH)]
 WORDS = FEAT // 2
 XBUFS = 8
-ROOT_ON_SCALAR_FROM = 6
+ROOT_ON_SCALAR_FROM = NCH - 5
 
 FLOPS = 2 * BATCH * FEAT * NODES * TREES + 2 * BATCH * LEAVES * TREES * OUTC
 

@@ -15,12 +15,13 @@ ADD = mybir.AluOpType.add
 P = 128
 BATCH, FEAT, TREES, NODES, LEAVES, OUTC = 8192, 1024, 128, 3, 4, 128
 ROWS = 4
-CHUNK_ROWS = [2] + [ROWS] * 15 + [2]
+CHUNK_ROWS = [2] * 3 + [ROWS] * 14 + [2]
 NCH = len(CHUNK_ROWS)
 FIRST_ROW = [P * sum(CHUNK_ROWS[:c]) for c in range(NCH)]
 WORDS = FEAT // 2
 XBUFS = 8
-ROOT_ON_SCALAR_FROM = NCH - 5
+ROOT_ON_SCALAR_FROM = NCH - 6
+ALL_ON_SCALAR_FROM = NCH - 2
 
 FLOPS = 2 * BATCH * FEAT * NODES * TREES + 2 * BATCH * LEAVES * TREES * OUTC
 
@@ -193,17 +194,19 @@ def tile_softtreeensemble_pa_t_kernel(tc, x, W, b, leaf_w, out):
                     bias=bias[:, n : n + 1],
                     scale=1.0,
                 )
-            if c >= ROOT_ON_SCALAR_FROM:
-                nc.scalar.activation(
-                    out=lines[:, 1:half:2, :],
-                    in_=z_t[c][0][:].rearrange("p (k i) -> p k i", i=4),
-                    func=SIGMOID,
-                    bias=minus_bias[:, 0:1],
-                    scale=-1.0,
-                )
+                if c >= (ROOT_ON_SCALAR_FROM if n == 0 else ALL_ON_SCALAR_FROM):
+                    nc.scalar.activation(
+                        out=lines[:, first + 1 : stop : step, :],
+                        in_=z_t[c][n][:].rearrange("p (k i) -> p k i", i=4),
+                        func=SIGMOID,
+                        bias=minus_bias[:, n : n + 1],
+                        scale=-1.0,
+                    )
             gh_t[c] = gh
 
         def complements(c):
+            if c >= ALL_ON_SCALAR_FROM:
+                return
             n_rows = P * CHUNK_ROWS[c]
             first = 2 * n_rows if c >= ROOT_ON_SCALAR_FROM else 0
             pairs = gh_t[c][:, first : 6 * n_rows].rearrange("p (k s i) -> p k s i", s=2, i=4)

@@ -15,13 +15,13 @@ ADD = mybir.AluOpType.add
 P = 128
 BATCH, FEAT, TREES, NODES, LEAVES, OUTC = 8192, 1024, 128, 3, 4, 128
 ROWS = 4
-CHUNK_ROWS = [2] * 3 + [ROWS] * 14 + [2]
+CHUNK_ROWS = [1, 1, 2, 2] + [ROWS] * 13 + [2, 2, 1, 1]
 NCH = len(CHUNK_ROWS)
 FIRST_ROW = [P * sum(CHUNK_ROWS[:c]) for c in range(NCH)]
 WORDS = FEAT // 2
 XBUFS = 8
-ROOT_ON_SCALAR_FROM = NCH - 6
-ALL_ON_SCALAR_FROM = NCH - 2
+ROOT_ON_SCALAR_FROM = 9
+ALL_ON_SCALAR_FROM = NCH
 
 FLOPS = 2 * BATCH * FEAT * NODES * TREES + 2 * BATCH * LEAVES * TREES * OUTC
 
@@ -124,13 +124,14 @@ def tile_softtreeensemble_pa_t_kernel(tc, x, W, b, leaf_w, out):
 
         def transposes(c):
             xw = x_t[c][:].bitcast(F32)
+            pair = min(CHUNK_ROWS[c], 2)
             banks = []
             for g in range(2):
-                for h in range(CHUNK_ROWS[c] // 2):
-                    xt = tps.tile([P, 2, 256], F32, tag="xt")
+                for h in range(CHUNK_ROWS[c] // pair):
+                    xt = tps.tile([P, 2, pair * P], F32, tag="xt")
                     for u in range(2):
-                        for q in range(2):
-                            off = (2 * h + q) * WORDS + 256 * g + 128 * u
+                        for q in range(pair):
+                            off = (pair * h + q) * WORDS + 256 * g + 128 * u
                             nc.tensor.transpose(
                                 xt[:, u, q * P : (q + 1) * P], xw[:, off : off + P], ident_f[:]
                             )
@@ -138,13 +139,15 @@ def tile_softtreeensemble_pa_t_kernel(tc, x, W, b, leaf_w, out):
             xt_t[c] = banks
 
         def leave_psum(c):
-            halves = CHUNK_ROWS[c] // 2
-            gx = gxp.tile([P, 1024 * halves], F32, tag="gx", align_bytes=64)
+            n_rows = P * CHUNK_ROWS[c]
+            per_bank = min(n_rows, 2 * P)
+            halves = n_rows // per_bank
+            gx = gxp.tile([P, 4 * n_rows], F32, tag="gx", align_bytes=64)
             gx4 = gx[:].rearrange("p (g c u) -> p g c u", g=2, u=2)
             for g in range(2):
                 for h in range(halves):
                     nc.scalar.copy(
-                        out=gx4[:, g, 256 * h : 256 * (h + 1), :],
+                        out=gx4[:, g, per_bank * h : per_bank * (h + 1), :],
                         in_=xt_t[c][halves * g + h][:].rearrange("p u c -> p c u"),
                     )
             gx_t[c] = gx
@@ -242,7 +245,10 @@ def tile_softtreeensemble_pa_t_kernel(tc, x, W, b, leaf_w, out):
 
         def leaves_matmul(c):
             pc, ps = pc_t[c]
-            o_ps = ops.tile([P, CHUNK_ROWS[c] * OUTC], F32, tag="o")
+            if c >= NCH - 4:
+                o_ps = tps.tile([P, CHUNK_ROWS[c] * OUTC], F32, tag="xt")
+            else:
+                o_ps = ops.tile([P, CHUNK_ROWS[c] * OUTC], F32, tag="o")
             for r in range(CHUNK_ROWS[c]):
                 col = slice(r * P, (r + 1) * P)
                 nc.tensor.matmul_mx(

@@ -68,11 +68,12 @@ def tile_softtreeensemble_pa_t_kernel(tc, x, W, b, leaf_w, out):
         load_x(0)
         nc.sync.dma_start(out=b_sb[0:NODES, :], in_=b)
         l_sb = const.tile([P, LEAVES * TREES], BF16)
-        nc.sync.dma_start(
-            out=l_sb[:].rearrange("c (j t) -> c j t", j=LEAVES),
-            in_=leaf_w.rearrange("j c t -> c j t"),
-        )
         for c in range(1, XBUFS):
+            if c == 4:
+                nc.sync.dma_start(
+                    out=l_sb[:].rearrange("c (j t) -> c j t", j=LEAVES),
+                    in_=leaf_w.rearrange("j c t -> c j t"),
+                )
             load_x(c)
 
         nc.scalar.activation(out=warm_out[:], in_=warm_in[:], func=SIGMOID)
@@ -107,11 +108,12 @@ def tile_softtreeensemble_pa_t_kernel(tc, x, W, b, leaf_w, out):
         ws = const.tile([P, NODES * 256], U8, align_bytes=64)
         for n in range(NODES):
             wt = tps.tile([P, 4, P], F32, tag="xt")
+            copy_out = nc.scalar.copy if n == 1 else nc.vector.tensor_copy
             for g in range(2):
                 for u in range(2):
                     off = n * WORDS + 256 * g + 128 * u
                     nc.tensor.transpose(wt[:, 2 * g + u, :], ww[:, off : off + P], ident_f[:])
-            nc.vector.tensor_copy(
+            copy_out(
                 out=wg[:, n * 512 : (n + 1) * 512].rearrange("p (g t u) -> p g t u", g=2, u=2),
                 in_=wt[:].rearrange("p (g u) t -> p g t u", u=2),
             )

@@ -15,12 +15,12 @@ ADD = mybir.AluOpType.add
 P = 128
 BATCH, FEAT, TREES, NODES, LEAVES, OUTC = 8192, 1024, 128, 3, 4, 128
 ROWS = 4
-CHUNK_ROWS = [1, 1, 2, 2] + [ROWS] * 13 + [2, 2, 1, 1]
+CHUNK_ROWS = [1, 1, 2, 2] + [ROWS] * 14 + [1, 1]
 NCH = len(CHUNK_ROWS)
 FIRST_ROW = [P * sum(CHUNK_ROWS[:c]) for c in range(NCH)]
 WORDS = FEAT // 2
 XBUFS = 8
-ROOT_ON_SCALAR_FROM = 9
+ROOT_ON_SCALAR_FROM = 10
 ALL_ON_SCALAR_FROM = NCH
 
 FLOPS = 2 * BATCH * FEAT * NODES * TREES + 2 * BATCH * LEAVES * TREES * OUTC
@@ -247,7 +247,7 @@ def tile_softtreeensemble_pa_t_kernel(tc, x, W, b, leaf_w, out):
 
         def leaves_matmul(c):
             pc, ps = pc_t[c]
-            if c >= NCH - 4:
+            if c >= NCH - 3:
                 o_ps = tps.tile([P, CHUNK_ROWS[c] * OUTC], F32, tag="xt")
             else:
                 o_ps = ops.tile([P, CHUNK_ROWS[c] * OUTC], F32, tag="o")

from contextlib import ExitStack

import concourse.mybir as mybir
from concourse.masks import make_identity

BF16 = mybir.dt.bfloat16
F32 = mybir.dt.float32
U32 = mybir.dt.uint32
U8 = mybir.dt.uint8
FP8X4 = mybir.dt.float8_e4m3fn_x4
SIGMOID = mybir.ActivationFunctionType.Sigmoid
MULT = mybir.AluOpType.mult
ADD = mybir.AluOpType.add

P = 128
BATCH, FEAT, TREES, NODES, LEAVES, OUTC = 8192, 1024, 128, 3, 4, 128
ROWS = 4
CHUNK_ROWS = [1, 1, 2, 2] + [ROWS] * 14 + [1, 1]
NCH = len(CHUNK_ROWS)
FIRST_ROW = [P * sum(CHUNK_ROWS[:c]) for c in range(NCH)]
WORDS = FEAT // 2
XBUFS = 8
ROOT_ON_SCALAR_FROM = 10
ALL_ON_SCALAR_FROM = NCH

FLOPS = 2 * BATCH * FEAT * NODES * TREES + 2 * BATCH * LEAVES * TREES * OUTC


def tile_softtreeensemble_pa_t_kernel(tc, x, W, b, leaf_w, out):
    nc = tc.nc
    with ExitStack() as ctx:
        const = ctx.enter_context(tc.tile_pool(name="const", bufs=1))
        xin = ctx.enter_context(tc.tile_pool(name="xin", bufs=XBUFS))
        gxp = ctx.enter_context(tc.tile_pool(name="gxp", bufs=3))
        xcp = ctx.enter_context(tc.tile_pool(name="xcp", bufs=2))
        ghp = ctx.enter_context(tc.tile_pool(name="ghp", bufs=3))
        pgp = ctx.enter_context(tc.tile_pool(name="pgp", bufs=2))
        osb = ctx.enter_context(tc.tile_pool(name="osb", bufs=4))
        tps = ctx.enter_context(tc.psum_pool(name="tps", bufs=4))
        zps = ctx.enter_context(tc.psum_pool(name="zps", bufs=3))
        ops = ctx.enter_context(tc.psum_pool(name="ops", bufs=1))

        x_t, xt_t, gx_t, xc_t, z_t, gh_t, pg_t, pc_t, o_t = {}, {}, {}, {}, {}, {}, {}, {}, {}

        def load_x(c):
            rows = CHUNK_ROWS[c]
            x_sb = xin.tile([P, rows * FEAT], BF16, tag="x")
            nc.sync.dma_start(
                out=x_sb[:],
                in_=x[FIRST_ROW[c] : FIRST_ROW[c] + P * rows, :].rearrange("(p r) d -> p (r d)", r=rows),
            )
            x_t[c] = x_sb

        ident_f = const.tile([P, P], F32)
        make_identity(nc, ident_f[:])
        ident_b = const.tile([P, P], BF16)
        make_identity(nc, ident_b[:])

        warm_in = const.tile([P, 1], F32)
        warm_out = const.tile([P, 1], F32)
        nc.vector.memset(warm_in[:], 0.0)
        b_sb = const.tile([P, P], BF16)
        nc.vector.memset(b_sb[:], 0.0)

        w_sb = const.tile([P, NODES * FEAT], BF16)
        for n in range(NODES):
            nc.sync.dma_start(out=w_sb[:, n * FEAT : (n + 1) * FEAT], in_=W[n, :, :])
        load_x(0)
        nc.sync.dma_start(out=b_sb[0:NODES, :], in_=b)
        l_sb = const.tile([P, LEAVES * TREES], BF16)
        for c in range(1, XBUFS):
            if c == 4:
                nc.sync.dma_start(
                    out=l_sb[:].rearrange("c (j t) -> c j t", j=LEAVES),
                    in_=leaf_w.rearrange("j c t -> c j t"),
                )
            load_x(c)

        nc.scalar.activation(out=warm_out[:], in_=warm_in[:], func=SIGMOID)

        bias = const.tile([P, NODES], F32)
        minus_bias = const.tile([P, NODES], F32)
        lg = const.tile([P, OUTC * LEAVES], BF16, align_bytes=64)
        lc = const.tile([P, OUTC], U32, align_bytes=64)
        ls = const.tile([P, OUTC], U8, align_bytes=64)

        def prepare_bias():
            bt = zps.tile([P, P], BF16, tag="z")
            nc.tensor.transpose(bt[:], b_sb[:], ident_b[:])
            nc.vector.tensor_copy(out=bias[:], in_=bt[:, 0:NODES])
            nc.vector.tensor_scalar(
                out=minus_bias[:], in0=bt[:, 0:NODES], scalar1=-1.0, scalar2=None, op0=MULT
            )

        def prepare_leaves():
            lt = ops.tile([P, LEAVES, OUTC], BF16, tag="o")
            for j in range(LEAVES):
                nc.tensor.transpose(lt[:, j, :], l_sb[:, j * TREES : (j + 1) * TREES], ident_b[:])
            nc.vector.tensor_copy(
                out=lg[:].rearrange("p (c j) -> p c j", j=LEAVES),
                in_=lt[:].rearrange("p j c -> p c j"),
            )
            nc.vector.quantize_mx(out=lc[:].bitcast(FP8X4), scales=ls[:], in_=lg[:])

        ww = w_sb[:].bitcast(F32)
        wg = const.tile([P, NODES * 512], F32, align_bytes=64)
        wc = const.tile([P, NODES * 256], U32, align_bytes=64)
        ws = const.tile([P, NODES * 256], U8, align_bytes=64)
        for n in range(NODES):
            wt = tps.tile([P, 4, P], F32, tag="xt")
            copy_out = nc.scalar.copy if n == 1 else nc.vector.tensor_copy
            for g in range(2):
                for u in range(2):
                    off = n * WORDS + 256 * g + 128 * u
                    nc.tensor.transpose(wt[:, 2 * g + u, :], ww[:, off : off + P], ident_f[:])
            copy_out(
                out=wg[:, n * 512 : (n + 1) * 512].rearrange("p (g t u) -> p g t u", g=2, u=2),
                in_=wt[:].rearrange("p (g u) t -> p g t u", u=2),
            )
        for n in range(NODES):
            nc.vector.quantize_mx(
                out=wc[:, n * 256 : (n + 1) * 256].bitcast(FP8X4),
                scales=ws[:, n * 256 : (n + 1) * 256],
                in_=wg[:].bitcast(BF16)[:, n * 1024 : (n + 1) * 1024],
            )

        def transposes(c):
            xw = x_t[c][:].bitcast(F32)
            pair = min(CHUNK_ROWS[c], 2)
            banks = []
            for g in range(2):
                for h in range(CHUNK_ROWS[c] // pair):
                    xt = tps.tile([P, 2, pair * P], F32, tag="xt")
                    for u in range(2):
                        for q in range(pair):
                            off = (pair * h + q) * WORDS + 256 * g + 128 * u
                            nc.tensor.transpose(
                                xt[:, u, q * P : (q + 1) * P], xw[:, off : off + P], ident_f[:]
                            )
                    banks.append(xt)
            xt_t[c] = banks

        def leave_psum(c):
            n_rows = P * CHUNK_ROWS[c]
            per_bank = min(n_rows, 2 * P)
            halves = n_rows // per_bank
            gx = gxp.tile([P, 4 * n_rows], F32, tag="gx", align_bytes=64)
            gx4 = gx[:].rearrange("p (g c u) -> p g c u", g=2, u=2)
            for g in range(2):
                for h in range(halves):
                    nc.scalar.copy(
                        out=gx4[:, g, per_bank * h : per_bank * (h + 1), :],
                        in_=xt_t[c][halves * g + h][:].rearrange("p u c -> p c u"),
                    )
            gx_t[c] = gx

        def quantise_x(c):
            cols = 2 * P * CHUNK_ROWS[c]
            xc = xcp.tile([P, cols], U32, tag="xc", align_bytes=64)
            xs = xcp.tile([P, cols], U8, tag="xs", align_bytes=64)
            nc.vector.quantize_mx(
                out=xc[:].bitcast(FP8X4), scales=xs[:], in_=gx_t[c][:].bitcast(BF16)
            )
            xc_t[c] = (xc, xs)

        def gates_matmul(c):
            xc, xs = xc_t[c]
            n_rows = P * CHUNK_ROWS[c]
            zs = []
            for n in range(NODES):
                z = zps.tile([P, n_rows], F32, tag="z")
                for g in range(2):
                    wcol = slice((2 * n + g) * P, (2 * n + g + 1) * P)
                    xcol = slice(g * n_rows, (g + 1) * n_rows)
                    nc.tensor.matmul_mx(
                        out=z[:],
                        lhsT=wc[:, wcol].bitcast(FP8X4),
                        lhsT_scale=ws[:, wcol],
                        rhs=xc[:, xcol].bitcast(FP8X4),
                        rhs_scale=xs[:, xcol],
                        start=(g == 0),
                        stop=(g == 1),
                    )
                zs.append(z)
            z_t[c] = zs

        def sigmoids(c):
            n_rows = P * CHUNK_ROWS[c]
            half = n_rows // 2
            gh = ghp.tile([P, 2 * NODES * n_rows], F32, tag="gh")
            lines = gh[:].rearrange("p (k i) -> p k i", i=4)
            for n in range(NODES):
                first, step = ((0, 2), (half, 4), (half + 2, 4))[n]
                stop = half if n == 0 else 3 * half
                nc.scalar.activation(
                    out=lines[:, first:stop:step, :],
                    in_=z_t[c][n][:].rearrange("p (k i) -> p k i", i=4),
                    func=SIGMOID,
                    bias=bias[:, n : n + 1],
                    scale=1.0,
                )
                if c >= (ROOT_ON_SCALAR_FROM if n == 0 else ALL_ON_SCALAR_FROM):
                    nc.scalar.activation(
                        out=lines[:, first + 1 : stop : step, :],
                        in_=z_t[c][n][:].rearrange("p (k i) -> p k i", i=4),
                        func=SIGMOID,
                        bias=minus_bias[:, n : n + 1],
                        scale=-1.0,
                    )
            gh_t[c] = gh

        def complements(c):
            if c >= ALL_ON_SCALAR_FROM:
                return
            n_rows = P * CHUNK_ROWS[c]
            first = 2 * n_rows if c >= ROOT_ON_SCALAR_FROM else 0
            pairs = gh_t[c][:, first : 6 * n_rows].rearrange("p (k s i) -> p k s i", s=2, i=4)
            nc.vector.tensor_scalar(
                out=pairs[:, :, 1:2, :],
                in0=pairs[:, :, 0:1, :],
                scalar1=-1.0,
                scalar2=1.0,
                op0=MULT,
                op1=ADD,
            )

        def products(c):
            gh = gh_t[c]
            n_rows = P * CHUNK_ROWS[c]
            pg = pgp.tile([P, n_rows * LEAVES], BF16, tag="pg", align_bytes=64)
            nc.vector.tensor_tensor(
                out=pg[:].rearrange("p (k i a b) -> p k a b i", i=4, a=2, b=2),
                in0=gh[:, 0 : 2 * n_rows]
                .rearrange("p (k a o i) -> p k a o i", a=2, o=1, i=4)
                .to_broadcast([P, n_rows // 4, 2, 2, 4]),
                in1=gh[:, 2 * n_rows : 6 * n_rows].rearrange("p (k a b i) -> p k a b i", a=2, b=2, i=4),
                op=MULT,
            )
            pg_t[c] = pg

        def quantise_p(c):
            n_rows = P * CHUNK_ROWS[c]
            pc = pgp.tile([P, n_rows], U32, tag="pc", align_bytes=64)
            ps = pgp.tile([P, n_rows], U8, tag="ps", align_bytes=64)
            nc.vector.quantize_mx(out=pc[:].bitcast(FP8X4), scales=ps[:], in_=pg_t[c][:])
            pc_t[c] = (pc, ps)

        def leaves_matmul(c):
            pc, ps = pc_t[c]
            if c >= NCH - 3:
                o_ps = tps.tile([P, CHUNK_ROWS[c] * OUTC], F32, tag="xt")
            else:
                o_ps = ops.tile([P, CHUNK_ROWS[c] * OUTC], F32, tag="o")
            for r in range(CHUNK_ROWS[c]):
                col = slice(r * P, (r + 1) * P)
                nc.tensor.matmul_mx(
                    out=o_ps[:, r * OUTC : (r + 1) * OUTC],
                    lhsT=pc[:, col].bitcast(FP8X4),
                    lhsT_scale=ps[:, col],
                    rhs=lc[:].bitcast(FP8X4),
                    rhs_scale=ls[:],
                    start=True,
                    stop=True,
                )
            o_t[c] = o_ps

        def store(c):
            rows = CHUNK_ROWS[c]
            o_sb = osb.tile([P, rows * OUTC], F32, tag="o_sb")
            nc.scalar.copy(out=o_sb[:], in_=o_t[c][:])
            nc.sync.dma_start(
                out=out[FIRST_ROW[c] : FIRST_ROW[c] + P * rows, :].rearrange("(p r) c -> p (r c)", r=rows),
                in_=o_sb[:],
            )

        def live(c):
            return 0 <= c < NCH

        for i in range(-3, NCH + 2):
            if live(i - 1):
                products(i - 1)
            if live(i + 1):
                gates_matmul(i + 1)
                sigmoids(i + 1)
            if live(i):
                complements(i)
            if live(i + 3):
                transposes(i + 3)
                leave_psum(i + 3)
                if live(i + 3 + XBUFS):
                    load_x(i + 3 + XBUFS)
            if i == -3:
                prepare_bias()
            if live(i - 2):
                leaves_matmul(i - 2)
                store(i - 2)
            if live(i + 2):
                quantise_x(i + 2)
            if i == -1:
                prepare_leaves()
            if live(i - 1):
                quantise_p(i - 1)
